import numpy as np
import ml_dtypes


def mxq(x, axis, fmt="e4m3"):
    dtype, down = {"e4m3": (ml_dtypes.float8_e4m3fn, 7), "e5m2": (ml_dtypes.float8_e5m2, 14)}[fmt]
    v = np.moveaxis(np.asarray(x, np.float32).astype(ml_dtypes.bfloat16).astype(np.float64), axis, -1)
    blocks = v.reshape(v.shape[:-1] + (-1, 32))
    amax = np.abs(blocks).max(-1, keepdims=True)
    byte = np.maximum(np.where(amax > 0, np.frexp(amax)[1] - 1 + 127, 0) - down, 1)
    scale = np.exp2(byte - 127.0)
    codes = (blocks / scale).astype(np.float32).astype(dtype).astype(np.float64)
    return np.moveaxis((codes * scale).reshape(v.shape), -1, axis)


WIDE = False


def mx_kscale(k):
    if not WIDE:
        return np.ones(k)
    levels = np.array([10, -10, 5, -5, 0])
    a = np.random.permutation(np.resize(levels, k // 512 * 4)).reshape(k // 512, 4)
    idx = np.arange(k)
    return np.exp2(a[idx // 512, idx % 128 // 32])


BF16 = ml_dtypes.bfloat16


def bf(x):
    return np.asarray(x, np.float32).astype(BF16)


def f64(x):
    return np.asarray(x).astype(np.float64)


E2M1 = np.array([0.0, 0.5, 1.0, 1.5, 2.0, 3.0, 4.0, 6.0, -0.0, -0.5, -1.0, -1.5, -2.0, -3.0, -4.0, -6.0])


def pack_weight(w, fmt):
    k, n = w.shape
    w = f64(bf(w)).reshape(k // 32, 32, n)
    amax = np.abs(w).max(1)
    if fmt == "e4m3":
        byte = np.frexp(amax)[1] - 1 + 127 - 7
    else:
        mant, ex = np.frexp(amax / 6.0)
        byte = np.where(mant > 0.5, ex, ex - 1) + 127
    byte = np.clip(np.where(amax > 0, byte, 1), 1, 254)
    scaled = (w * np.exp2(127.0 - byte)[:, None, :]).reshape(k, n).astype(np.float32)
    by_word = np.ascontiguousarray(scaled.reshape(k // 512, 128, 4, n).transpose(0, 1, 3, 2))
    if fmt == "e4m3":
        words = by_word.astype(ml_dtypes.float8_e4m3fn).view(np.uint8)
    else:
        c = by_word.astype(ml_dtypes.float4_e2m1fn).view(np.uint8) & 0xF
        words = c[..., 0::2] | (c[..., 1::2] << 4)
    return np.ascontiguousarray(words), np.ascontiguousarray(byte.astype(np.uint8).reshape(k // 512, 16, n))


def unpack_weight(words, scales, fmt):
    g, p, n, _ = words.shape
    if fmt == "e4m3":
        vals = np.ascontiguousarray(words).view(ml_dtypes.float8_e4m3fn).astype(np.float64)
    else:
        nib = np.empty((g, p, n, 4), np.uint8)
        nib[..., 0::2] = words & 0xF
        nib[..., 1::2] = words >> 4
        vals = E2M1[nib]
    vals = vals * np.repeat(np.exp2(scales.astype(np.float64) - 127.0), 8, axis=1)[..., None]
    return vals.transpose(0, 1, 3, 2).reshape(g * 512, n)

def pack4(w):
    words, scales = pack_weight(w, "e2m1")
    return words.reshape(words.shape[0], 128, -1), scales


def unpack4(words, scales):
    return unpack_weight(words.reshape(words.shape[0], 128, -1, 2), scales, "e2m1")


C_COUNT, NC, ROW, COL = 4, 48, 1024, 256


def setup_inputs():
    s = mx_kscale(ROW)
    Pb = bf(np.random.standard_normal((C_COUNT, ROW, ROW)) * 1.25 / np.sqrt(ROW))
    Ev = bf(np.random.standard_normal((C_COUNT, ROW, ROW)) * s)
    stack = np.random.standard_normal((C_COUNT, ROW, ROW)) / np.sqrt(ROW) / s[:, None]
    words, scales = pack4(stack.reshape(-1, ROW))
    feat = bf(np.random.standard_normal((C_COUNT, ROW, COL)))
    return {"Pb": Pb, "Ev": Ev, "W_pie_words": words, "W_pie_scales": scales, "feat": feat}


def reference(Pb, Ev, W_pie_words, W_pie_scales, feat):
    W = unpack4(W_pie_words, W_pie_scales).reshape(C_COUNT, ROW, ROW)
    T = mxq(f64(Ev), 2, "e4m3") @ W
    d = (f64(Pb) * T.transpose(0, 2, 1)).sum(-1)
    return 0.3 * d[:, :, None] * f64(feat) + f64(feat)

@@ -1,0 +1,198 @@
+from contextlib import ExitStack
+
+import concourse.mybir as mybir
+from concourse.masks import make_identity
+
+F32 = mybir.dt.float32
+BF16 = mybir.dt.bfloat16
+U8 = mybir.dt.uint8
+U32 = mybir.dt.uint32
+I32 = mybir.dt.int32
+FP8X4 = mybir.dt.float8_e4m3fn_x4
+FP4X4 = mybir.dt.float4_e2m1fn_x4
+MULT = mybir.AluOpType.mult
+ADD = mybir.AluOpType.add
+COPY = mybir.ActivationFunctionType.Copy
+
+P = 128
+C_COUNT = 4
+ROW = 1024
+COL = 256
+K_PASS = 4 * P
+PASSES = ROW // K_PASS
+J_UNIT = 512
+HALVES = ROW // J_UNIT
+UNITS = C_COUNT * HALVES
+ROWS_PER_PARTITION = J_UNIT // P
+I_TILES = ROW // P
+I_TILES_PER_LOAD = 2
+RESIDUAL_SCALE = 0.3
+
+FLOPS = 2 * C_COUNT * ROW * ROW * ROW
+
+
+def tile_generator_pa_t_e_kernel(tc, Pb, Ev, W_pie_words, W_pie_scales, feat, out):
+    nc = tc.nc
+
+    ev_rows = Ev.rearrange("c (h r a) k -> c h r (a k)", h=HALVES, a=ROWS_PER_PARTITION)
+    pb_rows = Pb.rearrange("c (t p) j -> c p t j", p=P)
+    feat_rows = feat.rearrange("c (t p) f -> c p t f", p=P)
+    out_rows = out.rearrange("c (t p) f -> c p t f", p=P)
+    w_word_rows = W_pie_words.bitcast(I32).rearrange("g p w -> p g w")
+    w_scale_rows = W_pie_scales.bitcast(I32).rearrange("g q n -> q g n")
+
+    with ExitStack() as ctx:
+        resident = ctx.enter_context(tc.tile_pool(name="resident", bufs=1))
+        ev_or_out = ctx.enter_context(tc.tile_pool(name="ev_or_out", bufs=UNITS))
+        staging = ctx.enter_context(tc.tile_pool(name="staging", bufs=2))
+        products = ctx.enter_context(tc.tile_pool(name="products", bufs=4))
+        psum = ctx.enter_context(tc.psum_pool(name="psum", bufs=4))
+        ctx.enter_context(tc.manual_schedule())
+
+        identity = resident.tile([P, P], F32, name="identity")
+        make_identity(nc, identity[:])
+
+        w_planes = resident.tile([P, C_COUNT * PASSES, ROW], U8, name="w_planes", align_bytes=64)
+        w_planes_i32 = w_planes[:].bitcast(I32)
+        nc.vector.memset(w_planes_i32, 0)
+
+        ev_sb = []
+        pb_sb = []
+        w_sb = []
+        feat_sb = []
+
+        def load_ev(c, h):
+            ev_tile = ev_or_out.tile([P, ROWS_PER_PARTITION, ROW], BF16, name="ev%d_%d" % (c, h), tag="ev_or_out")
+            nc.sync.dma_start(out=ev_tile[:].rearrange("p a k -> p (a k)"), in_=ev_rows[c, h])
+            ev_sb.append(ev_tile)
+
+        def load_pb(c, first_tile, last_tile):
+            for t in range(first_tile, last_tile, I_TILES_PER_LOAD):
+                pb_tile = resident.tile([P, I_TILES_PER_LOAD, ROW], BF16, name="pb%d_%d" % (c, t))
+                nc.sync.dma_start(out=pb_tile[:], in_=pb_rows[c, :, t : t + I_TILES_PER_LOAD, :])
+                pb_sb.append(pb_tile)
+
+        def load_w_scales():
+            for pass_half in range(2):
+                some_passes = slice(4 * pass_half, 4 * pass_half + 4)
+                for q in range(8):
+                    partition = 32 * (q // 4) + q % 4
+                    nc.sync.dma_start(
+                        out=w_planes_i32[partition:P:64, some_passes, :],
+                        in_=w_scale_rows[q:16:8, some_passes, :],
+                    )
+
+        def load_w_words(c):
+            w_tile = resident.tile([P, PASSES, 2 * ROW], U8, name="w%d" % c, align_bytes=64)
+            nc.sync.dma_start(out=w_tile[:].bitcast(I32), in_=w_word_rows[:, PASSES * c : PASSES * (c + 1), :])
+            w_sb.append(w_tile)
+
+        def load_feat(c):
+            feat_tile = resident.tile([P, I_TILES, COL], BF16, name="feat%d" % c)
+            half = I_TILES // 2
+            nc.sync.dma_start(out=feat_tile[:, :half, :], in_=feat_rows[c, :, :half, :])
+            nc.sync.dma_start(out=feat_tile[:, half:, :], in_=feat_rows[c, :, half:, :])
+            feat_sb.append(feat_tile)
+
+        for c in range(C_COUNT):
+            load_ev(c, 0)
+            if c == 0:
+                load_w_scales()
+            load_w_words(c)
+            load_pb(c, 0, I_TILES // 2)
+            load_ev(c, 1)
+            load_pb(c, I_TILES // 2, I_TILES)
+            load_feat(c)
+
+        d_parts = resident.tile([P, C_COUNT * I_TILES * HALVES], F32, name="d_parts")
+        factor = resident.tile([P, C_COUNT * I_TILES], F32, name="factor")
+
+        def transpose_and_quantise(unit):
+            ev_words = ev_sb[unit][:].bitcast(F32)
+            grouped = staging.tile([P, PASSES, 4 * J_UNIT], BF16, name="grouped", align_bytes=64)
+            grouped_words = grouped[:].bitcast(F32).rearrange("p g (r a_pair x) -> p g r a_pair x", a_pair=2, x=4)
+            codes = staging.tile([P, PASSES, J_UNIT], U32, name="codes", align_bytes=64)
+            planes = staging.tile([P, PASSES, J_UNIT], U8, name="planes", align_bytes=64)
+            for g in range(PASSES):
+                for a_pair in range(2):
+                    transposed = psum.tile([P, 4, P], F32, name="transposed")
+                    for a_low in range(2):
+                        for s in range(2):
+                            nc.tensor.transpose(
+                                transposed[:, 2 * a_low + s, :],
+                                ev_words[:, 2 * a_pair + a_low, 256 * g + s : 256 * (g + 1) : 2],
+                                identity[:],
+                            )
+                    nc.scalar.copy(
+                        out=grouped_words[:, g, :, a_pair, :],
+                        in_=transposed[:].rearrange("p x r -> p r x"),
+                    )
+            for g in range(PASSES):
+                nc.vector.quantize_mx(
+                    out=codes[:, g, :].bitcast(FP8X4),
+                    scales=planes[:, g, :],
+                    in_=grouped[:, g, :],
+                )
+            return codes, planes
+
+        def multiply_and_reduce(unit, quantised_ev, first_tile, last_tile):
+            c, h = divmod(unit, HALVES)
+            codes, planes = quantised_ev
+            for t in range(first_tile, last_tile):
+                t_transposed = psum.tile([P, J_UNIT], F32, name="t_transposed")
+                for g in range(PASSES):
+                    nc.tensor.matmul_mx(
+                        out=t_transposed[:],
+                        lhsT=w_sb[c][:, g, 2 * P * t : 2 * P * (t + 1)].bitcast(FP4X4),
+                        lhsT_scale=w_planes[:, PASSES * c + g, P * t : P * (t + 1)],
+                        rhs=codes[:, g, :].bitcast(FP8X4),
+                        rhs_scale=planes[:, g, :],
+                        start=(g == 0),
+                        stop=(g == PASSES - 1),
+                    )
+                pb_tile = pb_sb[(c * I_TILES + t) // I_TILES_PER_LOAD]
+                column = (c * I_TILES + t) * HALVES + h
+                product = products.tile([P, J_UNIT], F32, name="product")
+                nc.vector.scalar_tensor_tensor(
+                    out=product[:],
+                    in0=t_transposed[:],
+                    scalar=RESIDUAL_SCALE,
+                    in1=pb_tile[:, t % I_TILES_PER_LOAD, J_UNIT * h : J_UNIT * (h + 1)],
+                    op0=MULT,
+                    op1=MULT,
+                    accum_out=d_parts[:, column : column + 1],
+                )
+
+        def scale_feat_and_store(c):
+            out_tile = ev_or_out.tile([P, I_TILES, COL], F32, name="out%d" % c, tag="ev_or_out")
+            for t in range(I_TILES):
+                column = c * I_TILES + t
+                nc.gpsimd.tensor_scalar(
+                    out=factor[:, column : column + 1],
+                    in0=d_parts[:, HALVES * column : HALVES * column + 1],
+                    scalar1=d_parts[:, HALVES * column + 1 : HALVES * column + 2],
+                    scalar2=1.0,
+                    op0=ADD,
+                    op1=ADD,
+                )
+                nc.scalar.activation(
+                    out=out_tile[:, t, :],
+                    in_=feat_sb[c][:, t, :],
+                    func=COPY,
+                    scale=factor[:, column : column + 1],
+                )
+                if t % I_TILES_PER_LOAD == I_TILES_PER_LOAD - 1:
+                    tiles = slice(t + 1 - I_TILES_PER_LOAD, t + 1)
+                    nc.sync.dma_start(out=out_rows[c, :, tiles, :], in_=out_tile[:, tiles, :])
+
+        quantised_ev = transpose_and_quantise(0)
+        for unit in range(UNITS):
+            c, h = divmod(unit, HALVES)
+            multiply_and_reduce(unit, quantised_ev, 0, I_TILES // 2)
+            if unit + 1 < UNITS:
+                next_quantised_ev = transpose_and_quantise(unit + 1)
+            if h == 0 and c > 0:
+                scale_feat_and_store(c - 1)
+            multiply_and_reduce(unit, quantised_ev, I_TILES // 2, I_TILES)
+            quantised_ev = next_quantised_ev
+        scale_feat_and_store(C_COUNT - 1)

@@ -44,9 +44,9 @@ def tile_generator_pa_t_e_kernel(tc, Pb, Ev, W_pie_words, W_pie_scales, feat, ou
     with ExitStack() as ctx:
         resident = ctx.enter_context(tc.tile_pool(name="resident", bufs=1))
         ev_or_out = ctx.enter_context(tc.tile_pool(name="ev_or_out", bufs=UNITS))
-        staging = ctx.enter_context(tc.tile_pool(name="staging", bufs=2))
-        products = ctx.enter_context(tc.tile_pool(name="products", bufs=4))
-        psum = ctx.enter_context(tc.psum_pool(name="psum", bufs=4))
+        staging = ctx.enter_context(tc.tile_pool(name="staging", bufs=4))
+        products = ctx.enter_context(tc.tile_pool(name="products", bufs=8))
+        psum = ctx.enter_context(tc.psum_pool(name="psum", bufs=8))
         ctx.enter_context(tc.manual_schedule())
 
         identity = resident.tile([P, P], F32, name="identity")
@@ -61,26 +61,30 @@ def tile_generator_pa_t_e_kernel(tc, Pb, Ev, W_pie_words, W_pie_scales, feat, ou
         w_sb = []
         feat_sb = []
 
-        def load_ev(c, h):
-            ev_tile = ev_or_out.tile([P, ROWS_PER_PARTITION, ROW], BF16, name="ev%d_%d" % (c, h), tag="ev_or_out")
-            nc.sync.dma_start(out=ev_tile[:].rearrange("p a k -> p (a k)"), in_=ev_rows[c, h])
+        def load_ev(unit, pieces):
+            c, h = divmod(unit, HALVES)
+            ev_tile = ev_or_out.tile([P, ROWS_PER_PARTITION, ROW], BF16, name="ev%d" % unit, tag="ev_or_out")
+            flat = ev_tile[:].rearrange("p a k -> p (a k)")
+            width = ROWS_PER_PARTITION * ROW // pieces
+            for piece in range(pieces):
+                columns = slice(piece * width, (piece + 1) * width)
+                nc.sync.dma_start(out=flat[:, columns], in_=ev_rows[c, h][:, columns])
             ev_sb.append(ev_tile)
 
-        def load_pb(c, first_tile, last_tile):
-            for t in range(first_tile, last_tile, I_TILES_PER_LOAD):
+        def load_pb(c):
+            for t in range(0, I_TILES, I_TILES_PER_LOAD):
                 pb_tile = resident.tile([P, I_TILES_PER_LOAD, ROW], BF16, name="pb%d_%d" % (c, t))
                 nc.sync.dma_start(out=pb_tile[:], in_=pb_rows[c, :, t : t + I_TILES_PER_LOAD, :])
                 pb_sb.append(pb_tile)
 
-        def load_w_scales():
-            for pass_half in range(2):
-                some_passes = slice(4 * pass_half, 4 * pass_half + 4)
-                for q in range(8):
-                    partition = 32 * (q // 4) + q % 4
-                    nc.sync.dma_start(
-                        out=w_planes_i32[partition:P:64, some_passes, :],
-                        in_=w_scale_rows[q:16:8, some_passes, :],
-                    )
+        def load_w_scales(first_pass, last_pass):
+            some_passes = slice(first_pass, last_pass)
+            for q in range(8):
+                partition = 32 * (q // 4) + q % 4
+                nc.sync.dma_start(
+                    out=w_planes_i32[partition:P:64, some_passes, :],
+                    in_=w_scale_rows[q:16:8, some_passes, :],
+                )
 
         def load_w_words(c):
             w_tile = resident.tile([P, PASSES, 2 * ROW], U8, name="w%d" % c, align_bytes=64)
@@ -88,34 +92,32 @@ def tile_generator_pa_t_e_kernel(tc, Pb, Ev, W_pie_words, W_pie_scales, feat, ou
             w_sb.append(w_tile)
 
         def load_feat(c):
-            feat_tile = resident.tile([P, I_TILES, COL], BF16, name="feat%d" % c)
-            half = I_TILES // 2
-            nc.sync.dma_start(out=feat_tile[:, :half, :], in_=feat_rows[c, :, :half, :])
-            nc.sync.dma_start(out=feat_tile[:, half:, :], in_=feat_rows[c, :, half:, :])
+            feat_tile = ev_or_out.tile([P, I_TILES, COL], BF16, name="feat%d" % c, tag="ev_or_out")
+            nc.sync.dma_start(out=feat_tile[:], in_=feat_rows[c])
             feat_sb.append(feat_tile)
 
-        for c in range(C_COUNT):
-            load_ev(c, 0)
-            if c == 0:
-                load_w_scales()
-            load_w_words(c)
-            load_pb(c, 0, I_TILES // 2)
-            load_ev(c, 1)
-            load_pb(c, I_TILES // 2, I_TILES)
-            load_feat(c)
+        load_ev(0, 2)
+        for unit in range(1, UNITS):
+            load_ev(unit, 1)
 
         d_parts = resident.tile([P, C_COUNT * I_TILES * HALVES], F32, name="d_parts")
         factor = resident.tile([P, C_COUNT * I_TILES], F32, name="factor")
 
         def transpose_and_quantise(unit):
             ev_words = ev_sb[unit][:].bitcast(F32)
-            grouped = staging.tile([P, PASSES, 4 * J_UNIT], BF16, name="grouped", align_bytes=64)
-            grouped_words = grouped[:].bitcast(F32).rearrange("p g (r a_pair x) -> p g r a_pair x", a_pair=2, x=4)
-            codes = staging.tile([P, PASSES, J_UNIT], U32, name="codes", align_bytes=64)
-            planes = staging.tile([P, PASSES, J_UNIT], U8, name="planes", align_bytes=64)
+            grouped = []
+            grouped_words = []
             for g in range(PASSES):
-                for a_pair in range(2):
-                    transposed = psum.tile([P, 4, P], F32, name="transposed")
+                grouped_g = staging.tile([P, 4 * J_UNIT], BF16, name="grouped", align_bytes=64)
+                grouped.append(grouped_g)
+                grouped_words.append(
+                    grouped_g[:].bitcast(F32).rearrange("p (r a_pair x) -> p r a_pair x", a_pair=2, x=4)
+                )
+            codes = resident.tile([P, PASSES, J_UNIT], U32, name="codes%d" % unit, align_bytes=64)
+            planes = resident.tile([P, PASSES, J_UNIT], U8, name="planes%d" % unit, align_bytes=64)
+            for a_pair in range(2):
+                for g in range(PASSES):
+                    transposed = psum.tile([P, 4, P], F32, name="transposed", tag="bank")
                     for a_low in range(2):
                         for s in range(2):
                             nc.tensor.transpose(
@@ -123,76 +125,85 @@ def tile_generator_pa_t_e_kernel(tc, Pb, Ev, W_pie_words, W_pie_scales, feat, ou
                                 ev_words[:, 2 * a_pair + a_low, 256 * g + s : 256 * (g + 1) : 2],
                                 identity[:],
                             )
-                    nc.scalar.copy(
-                        out=grouped_words[:, g, :, a_pair, :],
-                        in_=transposed[:].rearrange("p x r -> p r x"),
-                    )
+                    if a_pair == 1 and g == PASSES - 1:
+                        nc.vector.tensor_copy(
+                            out=grouped_words[g][:, :, a_pair, :],
+                            in_=transposed[:].rearrange("p x r -> p r x"),
+                        )
+                    else:
+                        nc.scalar.copy(
+                            out=grouped_words[g][:, :, a_pair, :],
+                            in_=transposed[:].rearrange("p x r -> p r x"),
+                        )
             for g in range(PASSES):
                 nc.vector.quantize_mx(
                     out=codes[:, g, :].bitcast(FP8X4),
                     scales=planes[:, g, :],
-                    in_=grouped[:, g, :],
+                    in_=grouped[g][:],
                 )
             return codes, planes
 
-        def multiply_and_reduce(unit, quantised_ev, first_tile, last_tile):
-            c, h = divmod(unit, HALVES)
+        def multiply_and_reduce(c, t, h, quantised_ev):
             codes, planes = quantised_ev
-            for t in range(first_tile, last_tile):
-                t_transposed = psum.tile([P, J_UNIT], F32, name="t_transposed")
-                for g in range(PASSES):
-                    nc.tensor.matmul_mx(
-                        out=t_transposed[:],
-                        lhsT=w_sb[c][:, g, 2 * P * t : 2 * P * (t + 1)].bitcast(FP4X4),
-                        lhsT_scale=w_planes[:, PASSES * c + g, P * t : P * (t + 1)],
-                        rhs=codes[:, g, :].bitcast(FP8X4),
-                        rhs_scale=planes[:, g, :],
-                        start=(g == 0),
-                        stop=(g == PASSES - 1),
-                    )
-                pb_tile = pb_sb[(c * I_TILES + t) // I_TILES_PER_LOAD]
-                column = (c * I_TILES + t) * HALVES + h
-                product = products.tile([P, J_UNIT], F32, name="product")
-                nc.vector.scalar_tensor_tensor(
-                    out=product[:],
-                    in0=t_transposed[:],
-                    scalar=RESIDUAL_SCALE,
-                    in1=pb_tile[:, t % I_TILES_PER_LOAD, J_UNIT * h : J_UNIT * (h + 1)],
-                    op0=MULT,
-                    op1=MULT,
-                    accum_out=d_parts[:, column : column + 1],
+            t_transposed = psum.tile([P, J_UNIT], F32, name="t_transposed", tag="bank")
+            for g in range(PASSES):
+                nc.tensor.matmul_mx(
+                    out=t_transposed[:],
+                    lhsT=w_sb[c][:, g, 2 * P * t : 2 * P * (t + 1)].bitcast(FP4X4),
+                    lhsT_scale=w_planes[:, PASSES * c + g, P * t : P * (t + 1)],
+                    rhs=codes[:, g, :].bitcast(FP8X4),
+                    rhs_scale=planes[:, g, :],
+                    start=(g == 0),
+                    stop=(g == PASSES - 1),
                 )
+            pb_tile = pb_sb[(c * I_TILES + t) // I_TILES_PER_LOAD]
+            column = (c * I_TILES + t) * HALVES + h
+            product = products.tile([P, J_UNIT], F32, name="product")
+            nc.vector.scalar_tensor_tensor(
+                out=product[:],
+                in0=t_transposed[:],
+                scalar=RESIDUAL_SCALE,
+                in1=pb_tile[:, t % I_TILES_PER_LOAD, J_UNIT * h : J_UNIT * (h + 1)],
+                op0=MULT,
+                op1=MULT,
+                accum_out=d_parts[:, column : column + 1],
+            )
 
-        def scale_feat_and_store(c):
+        def scale_feat(c, t, out_tile):
+            column = c * I_TILES + t
+            nc.gpsimd.tensor_scalar(
+                out=factor[:, column : column + 1],
+                in0=d_parts[:, HALVES * column : HALVES * column + 1],
+                scalar1=d_parts[:, HALVES * column + 1 : HALVES * column + 2],
+                scalar2=1.0,
+                op0=ADD,
+                op1=ADD,
+            )
+            nc.scalar.activation(
+                out=out_tile[:, t, :],
+                in_=feat_sb[c][:, t, :],
+                func=COPY,
+                scale=factor[:, column : column + 1],
+            )
+
+        quantised = []
+        for unit in range(UNITS):
+            quantised.append(transpose_and_quantise(unit))
+        load_w_scales(0, PASSES)
+        load_w_words(0)
+        load_pb(0)
+        load_w_scales(PASSES, C_COUNT * PASSES)
+        for c in range(1, C_COUNT):
+            load_w_words(c)
+            load_pb(c)
+            load_feat(c - 1)
+        load_feat(C_COUNT - 1)
+        for c in range(C_COUNT):
             out_tile = ev_or_out.tile([P, I_TILES, COL], F32, name="out%d" % c, tag="ev_or_out")
             for t in range(I_TILES):
-                column = c * I_TILES + t
-                nc.gpsimd.tensor_scalar(
-                    out=factor[:, column : column + 1],
-                    in0=d_parts[:, HALVES * column : HALVES * column + 1],
-                    scalar1=d_parts[:, HALVES * column + 1 : HALVES * column + 2],
-                    scalar2=1.0,
-                    op0=ADD,
-                    op1=ADD,
-                )
-                nc.scalar.activation(
-                    out=out_tile[:, t, :],
-                    in_=feat_sb[c][:, t, :],
-                    func=COPY,
-                    scale=factor[:, column : column + 1],
-                )
+                for h in range(HALVES):
+                    multiply_and_reduce(c, t, h, quantised[c * HALVES + h])
+                scale_feat(c, t, out_tile)
                 if t % I_TILES_PER_LOAD == I_TILES_PER_LOAD - 1:
                     tiles = slice(t + 1 - I_TILES_PER_LOAD, t + 1)
                     nc.sync.dma_start(out=out_rows[c, :, tiles, :], in_=out_tile[:, tiles, :])
-
-        quantised_ev = transpose_and_quantise(0)
-        for unit in range(UNITS):
-            c, h = divmod(unit, HALVES)
-            multiply_and_reduce(unit, quantised_ev, 0, I_TILES // 2)
-            if unit + 1 < UNITS:
-                next_quantised_ev = transpose_and_quantise(unit + 1)
-            if h == 0 and c > 0:
-                scale_feat_and_store(c - 1)
-            multiply_and_reduce(unit, quantised_ev, I_TILES // 2, I_TILES)
-            quantised_ev = next_quantised_ev
-        scale_feat_and_store(C_COUNT - 1)

@@ -13,6 +13,7 @@ FP4X4 = mybir.dt.float4_e2m1fn_x4
 MULT = mybir.AluOpType.mult
 ADD = mybir.AluOpType.add
 COPY = mybir.ActivationFunctionType.Copy
+AXIS_X = mybir.AxisListType.X
 
 P = 128
 C_COUNT = 4
@@ -46,6 +47,7 @@ def tile_generator_pa_t_e_kernel(tc, Pb, Ev, W_pie_words, W_pie_scales, feat, ou
         ev_or_out = ctx.enter_context(tc.tile_pool(name="ev_or_out", bufs=UNITS))
         staging = ctx.enter_context(tc.tile_pool(name="staging", bufs=4))
         products = ctx.enter_context(tc.tile_pool(name="products", bufs=8))
+        elsewhere = ctx.enter_context(tc.tile_pool(name="elsewhere", bufs=2))
         psum = ctx.enter_context(tc.psum_pool(name="psum", bufs=8))
         ctx.enter_context(tc.manual_schedule())
 
@@ -100,7 +102,8 @@ def tile_generator_pa_t_e_kernel(tc, Pb, Ev, W_pie_words, W_pie_scales, feat, ou
         for unit in range(1, UNITS):
             load_ev(unit, 1)
 
-        d_parts = resident.tile([P, C_COUNT * I_TILES * HALVES], F32, name="d_parts")
+        d_parts = resident.tile([P, C_COUNT * I_TILES, HALVES + 1], F32, name="d_parts")
+        nc.vector.memset(d_parts[:], 1.0)
         factor = resident.tile([P, C_COUNT * I_TILES], F32, name="factor")
 
         def transpose_and_quantise(unit):
@@ -143,7 +146,7 @@ def tile_generator_pa_t_e_kernel(tc, Pb, Ev, W_pie_words, W_pie_scales, feat, ou
                 )
             return codes, planes
 
-        def multiply_and_reduce(c, t, h, quantised_ev):
+        def multiply(c, t, h, quantised_ev):
             codes, planes = quantised_ev
             t_transposed = psum.tile([P, J_UNIT], F32, name="t_transposed", tag="bank")
             for g in range(PASSES):
@@ -156,35 +159,58 @@ def tile_generator_pa_t_e_kernel(tc, Pb, Ev, W_pie_words, W_pie_scales, feat, ou
                     start=(g == 0),
                     stop=(g == PASSES - 1),
                 )
+            return t_transposed
+
+        def pb_half(c, t, h):
             pb_tile = pb_sb[(c * I_TILES + t) // I_TILES_PER_LOAD]
-            column = (c * I_TILES + t) * HALVES + h
+            return pb_tile[:, t % I_TILES_PER_LOAD, J_UNIT * h : J_UNIT * (h + 1)]
+
+        def d_column(c, t, h):
+            return d_parts[:, c * I_TILES + t, h : h + 1]
+
+        def reduce_on_vector(c, t, h, t_transposed):
             product = products.tile([P, J_UNIT], F32, name="product")
             nc.vector.scalar_tensor_tensor(
                 out=product[:],
                 in0=t_transposed[:],
                 scalar=RESIDUAL_SCALE,
-                in1=pb_tile[:, t % I_TILES_PER_LOAD, J_UNIT * h : J_UNIT * (h + 1)],
+                in1=pb_half(c, t, h),
                 op0=MULT,
                 op1=MULT,
-                accum_out=d_parts[:, column : column + 1],
+                accum_out=d_column(c, t, h),
             )
 
-        def scale_feat(c, t, out_tile):
-            column = c * I_TILES + t
-            nc.gpsimd.tensor_scalar(
-                out=factor[:, column : column + 1],
-                in0=d_parts[:, HALVES * column : HALVES * column + 1],
-                scalar1=d_parts[:, HALVES * column + 1 : HALVES * column + 2],
-                scalar2=1.0,
-                op0=ADD,
-                op1=ADD,
-            )
+        def start_reduce_elsewhere(c, t, h, t_transposed):
+            t_copy = elsewhere.tile([P, J_UNIT], F32, name="t_copy")
+            nc.scalar.copy(out=t_copy[:], in_=t_transposed[:])
+            t_product = elsewhere.tile([P, J_UNIT], F32, name="t_product")
+            nc.gpsimd.tensor_tensor(out=t_product[:], in0=t_copy[:], in1=pb_half(c, t, h), op=MULT)
+            return t_product
+
+        def finish_reduce_elsewhere(c, t, h, t_product):
             nc.scalar.activation(
-                out=out_tile[:, t, :],
-                in_=feat_sb[c][:, t, :],
+                out=t_product[:],
+                in_=t_product[:],
                 func=COPY,
-                scale=factor[:, column : column + 1],
+                scale=RESIDUAL_SCALE,
+                accum_out=d_column(c, t, h),
             )
+
+        def make_factors(c, first_tile, tiles):
+            columns = slice(c * I_TILES + first_tile, c * I_TILES + first_tile + tiles)
+            nc.vector.tensor_reduce(out=factor[:, columns], in_=d_parts[:, columns, :], axis=AXIS_X, op=ADD)
+
+        def scale_feat_and_store(c, first_tile):
+            tiles = slice(first_tile, first_tile + I_TILES_PER_LOAD)
+            for t in range(first_tile, first_tile + I_TILES_PER_LOAD):
+                column = c * I_TILES + t
+                nc.scalar.activation(
+                    out=out_sb[c][:, t, :],
+                    in_=feat_sb[c][:, t, :],
+                    func=COPY,
+                    scale=factor[:, column : column + 1],
+                )
+            nc.sync.dma_start(out=out_rows[c, :, tiles, :], in_=out_sb[c][:, tiles, :])
 
         quantised = []
         for unit in range(UNITS):
@@ -198,12 +224,31 @@ def tile_generator_pa_t_e_kernel(tc, Pb, Ev, W_pie_words, W_pie_scales, feat, ou
             load_pb(c)
             load_feat(c - 1)
         load_feat(C_COUNT - 1)
+
+        out_sb = []
         for c in range(C_COUNT):
             out_tile = ev_or_out.tile([P, I_TILES, COL], F32, name="out%d" % c, tag="ev_or_out")
-            for t in range(I_TILES):
+            out_sb.append(out_tile)
+
+        steps = [(c, t) for c in range(C_COUNT) for t in range(0, I_TILES, I_TILES_PER_LOAD)]
+        started = []
+        for step, (c, first_tile) in enumerate(steps):
+            newly_started = []
+            for t in range(first_tile, first_tile + I_TILES_PER_LOAD):
                 for h in range(HALVES):
-                    multiply_and_reduce(c, t, h, quantised[c * HALVES + h])
-                scale_feat(c, t, out_tile)
-                if t % I_TILES_PER_LOAD == I_TILES_PER_LOAD - 1:
-                    tiles = slice(t + 1 - I_TILES_PER_LOAD, t + 1)
-                    nc.sync.dma_start(out=out_rows[c, :, tiles, :], in_=out_tile[:, tiles, :])
+                    t_transposed = multiply(c, t, h, quantised[c * HALVES + h])
+                    last_bank = t == first_tile + I_TILES_PER_LOAD - 1 and h == HALVES - 1
+                    if last_bank and step < len(steps) - 1:
+                        newly_started.append((c, t, h, start_reduce_elsewhere(c, t, h, t_transposed)))
+                    else:
+                        reduce_on_vector(c, t, h, t_transposed)
+                if t == first_tile and step >= 2:
+                    make_factors(steps[step - 2][0], steps[step - 2][1], I_TILES_PER_LOAD)
+            for args in started:
+                finish_reduce_elsewhere(*args)
+            started = newly_started
+            if step >= 2:
+                scale_feat_and_store(*steps[step - 2])
+        make_factors(steps[-2][0], steps[-2][1], 2 * I_TILES_PER_LOAD)
+        scale_feat_and_store(*steps[-2])
+        scale_feat_and_store(*steps[-1])

@@ -79,14 +79,9 @@ def tile_generator_pa_t_e_kernel(tc, Pb, Ev, W_pie_words, W_pie_scales, feat, ou
                 nc.sync.dma_start(out=pb_tile[:], in_=pb_rows[c, :, t : t + I_TILES_PER_LOAD, :])
                 pb_sb.append(pb_tile)
 
-        def load_w_scales(first_pass, last_pass):
-            some_passes = slice(first_pass, last_pass)
-            for q in range(8):
-                partition = 32 * (q // 4) + q % 4
-                nc.sync.dma_start(
-                    out=w_planes_i32[partition:P:64, some_passes, :],
-                    in_=w_scale_rows[q:16:8, some_passes, :],
-                )
+        def load_w_scales():
+            for r in range(4):
+                nc.sync.dma_start(out=w_planes_i32[r:P:32, :, :], in_=w_scale_rows[r:16:4, :, :])
 
         def load_w_words(c):
             w_tile = resident.tile([P, PASSES, 2 * ROW], U8, name="w%d" % c, align_bytes=64)
@@ -99,7 +94,9 @@ def tile_generator_pa_t_e_kernel(tc, Pb, Ev, W_pie_words, W_pie_scales, feat, ou
             feat_sb.append(feat_tile)
 
         load_ev(0, 2)
-        for unit in range(1, UNITS):
+        load_ev(1, 1)
+        load_w_scales()
+        for unit in range(2, UNITS):
             load_ev(unit, 1)
 
         d_parts = resident.tile([P, C_COUNT * I_TILES, HALVES + 1], F32, name="d_parts")
@@ -215,10 +212,8 @@ def tile_generator_pa_t_e_kernel(tc, Pb, Ev, W_pie_words, W_pie_scales, feat, ou
         quantised = []
         for unit in range(UNITS):
             quantised.append(transpose_and_quantise(unit))
-        load_w_scales(0, PASSES)
         load_w_words(0)
         load_pb(0)
-        load_w_scales(PASSES, C_COUNT * PASSES)
         for c in range(1, C_COUNT):
             load_w_words(c)
             load_pb(c)

@@ -28,6 +28,7 @@ ROWS_PER_PARTITION = J_UNIT // P
 I_TILES = ROW // P
 I_TILES_PER_LOAD = 2
 RESIDUAL_SCALE = 0.3
+MOVED = C_COUNT - 1
 
 FLOPS = 2 * C_COUNT * ROW * ROW * ROW
 
@@ -39,6 +40,8 @@ def tile_generator_pa_t_e_kernel(tc, Pb, Ev, W_pie_words, W_pie_scales, feat, ou
     pb_rows = Pb.rearrange("c (t p) j -> c p t j", p=P)
     feat_rows = feat.rearrange("c (t p) f -> c p t f", p=P)
     out_rows = out.rearrange("c (t p) f -> c p t f", p=P)
+    feat_runs = feat.rearrange("c (p a) f -> c p a f", a=I_TILES)
+    out_runs = out.rearrange("c (p a) f -> c p a f", a=I_TILES)
     w_word_rows = W_pie_words.bitcast(I32).rearrange("g p w -> p g w")
     w_scale_rows = W_pie_scales.bitcast(I32).rearrange("g q n -> q g n")
 
@@ -53,6 +56,15 @@ def tile_generator_pa_t_e_kernel(tc, Pb, Ev, W_pie_words, W_pie_scales, feat, ou
 
         identity = resident.tile([P, P], F32, name="identity")
         make_identity(nc, identity[:])
+
+        group_of = resident.tile([P, P // I_TILES], F32, name="group_of")
+        nc.vector.tensor_reduce(
+            out=group_of[:], in_=identity[:].rearrange("p (q a) -> p q a", a=I_TILES), axis=AXIS_X, op=ADD
+        )
+        place_in_group = resident.tile([P, I_TILES], F32, name="place_in_group")
+        nc.vector.tensor_reduce(
+            out=place_in_group[:], in_=identity[:].rearrange("p (q a) -> p a q", a=I_TILES), axis=AXIS_X, op=ADD
+        )
 
         w_planes = resident.tile([P, C_COUNT * PASSES, ROW], U8, name="w_planes", align_bytes=64)
         w_planes_i32 = w_planes[:].bitcast(I32)
@@ -90,7 +102,7 @@ def tile_generator_pa_t_e_kernel(tc, Pb, Ev, W_pie_words, W_pie_scales, feat, ou
 
         def load_feat(c):
             feat_tile = ev_or_out.tile([P, I_TILES, COL], BF16, name="feat%d" % c, tag="ev_or_out")
-            nc.sync.dma_start(out=feat_tile[:], in_=feat_rows[c])
+            nc.sync.dma_start(out=feat_tile[:], in_=feat_runs[c] if c < MOVED else feat_rows[c])
             feat_sb.append(feat_tile)
 
         load_ev(0, 2)
@@ -197,16 +209,61 @@ def tile_generator_pa_t_e_kernel(tc, Pb, Ev, W_pie_words, W_pie_scales, feat, ou
             columns = slice(c * I_TILES + first_tile, c * I_TILES + first_tile + tiles)
             nc.vector.tensor_reduce(out=factor[:, columns], in_=d_parts[:, columns, :], axis=AXIS_X, op=ADD)
 
-        def scale_feat_and_store(c, first_tile):
+        factor_by_run = resident.tile([P, C_COUNT * I_TILES], F32, name="factor_by_run")
+
+        def spread_factors(c):
+            make_factors(c, 0, I_TILES)
+            spread = resident.tile([P, I_TILES, P // I_TILES], F32, name="spread%d" % c)
+            shape = [P, I_TILES, P // I_TILES]
+            nc.vector.tensor_tensor(
+                out=spread[:],
+                in0=factor[:, c * I_TILES : (c + 1) * I_TILES].unsqueeze(2).to_broadcast(shape),
+                in1=group_of[:].unsqueeze(1).to_broadcast(shape),
+                op=MULT,
+            )
+            return spread
+
+        def move_factors(c, spread):
+            moved = psum.tile([P, I_TILES], F32, name="moved", tag="bank")
+            nc.tensor.matmul(
+                out=moved[:],
+                lhsT=spread[:].rearrange("p t q -> p (t q)"),
+                rhs=place_in_group[:],
+                start=True,
+                stop=True,
+            )
+            nc.scalar.copy(out=factor_by_run[:, c * I_TILES : (c + 1) * I_TILES], in_=moved[:])
+
+        def scale_runs(c, first, last):
+            for a in range(first, last):
+                column = c * I_TILES + a
+                nc.scalar.activation(
+                    out=out_sb[c][:, a, :],
+                    in_=feat_sb[c][:, a, :],
+                    func=COPY,
+                    scale=factor_by_run[:, column : column + 1],
+                )
+
+        def store_runs(c, first, last):
+            nc.sync.dma_start(out=out_runs[c, :, first:last, :], in_=out_sb[c][:, first:last, :])
+
+        def scale_feat_and_store(c, first_tile, on_vector=False):
             tiles = slice(first_tile, first_tile + I_TILES_PER_LOAD)
             for t in range(first_tile, first_tile + I_TILES_PER_LOAD):
                 column = c * I_TILES + t
-                nc.scalar.activation(
-                    out=out_sb[c][:, t, :],
-                    in_=feat_sb[c][:, t, :],
-                    func=COPY,
-                    scale=factor[:, column : column + 1],
-                )
+                if on_vector:
+                    nc.vector.tensor_scalar_mul(
+                        out=out_sb[c][:, t, :],
+                        in0=feat_sb[c][:, t, :],
+                        scalar1=factor[:, column : column + 1],
+                    )
+                else:
+                    nc.scalar.activation(
+                        out=out_sb[c][:, t, :],
+                        in_=feat_sb[c][:, t, :],
+                        func=COPY,
+                        scale=factor[:, column : column + 1],
+                    )
             nc.sync.dma_start(out=out_rows[c, :, tiles, :], in_=out_sb[c][:, tiles, :])
 
         quantised = []
@@ -227,23 +284,38 @@ def tile_generator_pa_t_e_kernel(tc, Pb, Ev, W_pie_words, W_pie_scales, feat, ou
 
         steps = [(c, t) for c in range(C_COUNT) for t in range(0, I_TILES, I_TILES_PER_LOAD)]
         started = []
+        spread_sb = {}
         for step, (c, first_tile) in enumerate(steps):
+            step_in_c = first_tile // I_TILES_PER_LOAD
             newly_started = []
             for t in range(first_tile, first_tile + I_TILES_PER_LOAD):
                 for h in range(HALVES):
                     t_transposed = multiply(c, t, h, quantised[c * HALVES + h])
                     last_bank = t == first_tile + I_TILES_PER_LOAD - 1 and h == HALVES - 1
-                    if last_bank and step < len(steps) - 1:
+                    if last_bank and step_in_c < 3 and step < len(steps) - 2:
                         newly_started.append((c, t, h, start_reduce_elsewhere(c, t, h, t_transposed)))
                     else:
                         reduce_on_vector(c, t, h, t_transposed)
-                if t == first_tile and step >= 2:
-                    make_factors(steps[step - 2][0], steps[step - 2][1], I_TILES_PER_LOAD)
+                if t == first_tile:
+                    if c >= 1 and step_in_c == 0:
+                        spread_sb[c - 1] = spread_factors(c - 1)
+                    if c >= 1 and step_in_c == 1:
+                        move_factors(c - 1, spread_sb[c - 1])
+                    if c == C_COUNT - 1 and step_in_c >= 2:
+                        make_factors(c, first_tile - 2 * I_TILES_PER_LOAD, I_TILES_PER_LOAD)
             for args in started:
                 finish_reduce_elsewhere(*args)
             started = newly_started
-            if step >= 2:
-                scale_feat_and_store(*steps[step - 2])
+            if c >= 1 and step_in_c == 1:
+                scale_runs(c - 1, 0, 3)
+            if c >= 1 and step_in_c == 2:
+                scale_runs(c - 1, 3, 6)
+                store_runs(c - 1, 0, 4)
+            if c >= 1 and step_in_c == 3:
+                scale_runs(c - 1, 6, 8)
+                store_runs(c - 1, 4, 8)
+            if c == C_COUNT - 1 and step_in_c >= 2:
+                scale_feat_and_store(c, first_tile - 2 * I_TILES_PER_LOAD)
         make_factors(steps[-2][0], steps[-2][1], 2 * I_TILES_PER_LOAD)
         scale_feat_and_store(*steps[-2])
-        scale_feat_and_store(*steps[-1])
+        scale_feat_and_store(*steps[-1], on_vector=True)

@@ -247,23 +247,24 @@ def tile_generator_pa_t_e_kernel(tc, Pb, Ev, W_pie_words, W_pie_scales, feat, ou
         def store_runs(c, first, last):
             nc.sync.dma_start(out=out_runs[c, :, first:last, :], in_=out_sb[c][:, first:last, :])
 
-        def scale_feat_and_store(c, first_tile, on_vector=False):
+        def scale_tile(c, t, on_vector=False):
+            column = c * I_TILES + t
+            if on_vector:
+                nc.vector.tensor_scalar_mul(
+                    out=out_sb[c][:, t, :],
+                    in0=feat_sb[c][:, t, :],
+                    scalar1=factor[:, column : column + 1],
+                )
+            else:
+                nc.scalar.activation(
+                    out=out_sb[c][:, t, :],
+                    in_=feat_sb[c][:, t, :],
+                    func=COPY,
+                    scale=factor[:, column : column + 1],
+                )
+
+        def store_pair(c, first_tile):
             tiles = slice(first_tile, first_tile + I_TILES_PER_LOAD)
-            for t in range(first_tile, first_tile + I_TILES_PER_LOAD):
-                column = c * I_TILES + t
-                if on_vector:
-                    nc.vector.tensor_scalar_mul(
-                        out=out_sb[c][:, t, :],
-                        in0=feat_sb[c][:, t, :],
-                        scalar1=factor[:, column : column + 1],
-                    )
-                else:
-                    nc.scalar.activation(
-                        out=out_sb[c][:, t, :],
-                        in_=feat_sb[c][:, t, :],
-                        func=COPY,
-                        scale=factor[:, column : column + 1],
-                    )
             nc.sync.dma_start(out=out_rows[c, :, tiles, :], in_=out_sb[c][:, tiles, :])
 
         quantised = []
@@ -301,21 +302,29 @@ def tile_generator_pa_t_e_kernel(tc, Pb, Ev, W_pie_words, W_pie_scales, feat, ou
                         spread_sb[c - 1] = spread_factors(c - 1)
                     if c >= 1 and step_in_c == 1:
                         move_factors(c - 1, spread_sb[c - 1])
-                    if c == C_COUNT - 1 and step_in_c >= 2:
-                        make_factors(c, first_tile - 2 * I_TILES_PER_LOAD, I_TILES_PER_LOAD)
+                    if c == C_COUNT - 1 and step_in_c == 2:
+                        make_factors(c, 0, 2)
+                    if c == C_COUNT - 1 and step_in_c == 3:
+                        make_factors(c, 2, 5)
             for args in started:
                 finish_reduce_elsewhere(*args)
             started = newly_started
             if c >= 1 and step_in_c == 1:
-                scale_runs(c - 1, 0, 3)
-            if c >= 1 and step_in_c == 2:
-                scale_runs(c - 1, 3, 6)
+                scale_runs(c - 1, 0, 4)
                 store_runs(c - 1, 0, 4)
-            if c >= 1 and step_in_c == 3:
-                scale_runs(c - 1, 6, 8)
+            if c >= 1 and step_in_c == 2:
+                scale_runs(c - 1, 4, 8)
                 store_runs(c - 1, 4, 8)
-            if c == C_COUNT - 1 and step_in_c >= 2:
-                scale_feat_and_store(c, first_tile - 2 * I_TILES_PER_LOAD)
-        make_factors(steps[-2][0], steps[-2][1], 2 * I_TILES_PER_LOAD)
-        scale_feat_and_store(*steps[-2])
-        scale_feat_and_store(*steps[-1], on_vector=True)
+            if c == C_COUNT - 1 and step_in_c == 2:
+                scale_tile(c, 0)
+                scale_tile(c, 1)
+                store_pair(c, 0)
+            if c == C_COUNT - 1 and step_in_c == 3:
+                for pair in (2, 4):
+                    scale_tile(c, pair)
+                    scale_tile(c, pair + 1)
+                    store_pair(c, pair)
+                scale_tile(c, 6)
+        make_factors(C_COUNT - 1, I_TILES - 1, 1)
+        scale_tile(C_COUNT - 1, I_TILES - 1, on_vector=True)
+        store_pair(C_COUNT - 1, I_TILES - 2)

@@ -91,9 +91,10 @@ def tile_generator_pa_t_e_kernel(tc, Pb, Ev, W_pie_words, W_pie_scales, feat, ou
                 nc.sync.dma_start(out=pb_tile[:], in_=pb_rows[c, :, t : t + I_TILES_PER_LOAD, :])
                 pb_sb.append(pb_tile)
 
-        def load_w_scales():
+        def load_w_scales(first_pass, last_pass):
+            some_passes = slice(first_pass, last_pass)
             for r in range(4):
-                nc.sync.dma_start(out=w_planes_i32[r:P:32, :, :], in_=w_scale_rows[r:16:4, :, :])
+                nc.sync.dma_start(out=w_planes_i32[r:P:32, some_passes, :], in_=w_scale_rows[r:16:4, some_passes, :])
 
         def load_w_words(c):
             w_tile = resident.tile([P, PASSES, 2 * ROW], U8, name="w%d" % c, align_bytes=64)
@@ -107,7 +108,7 @@ def tile_generator_pa_t_e_kernel(tc, Pb, Ev, W_pie_words, W_pie_scales, feat, ou
 
         load_ev(0, 2)
         load_ev(1, 1)
-        load_w_scales()
+        load_w_scales(0, PASSES)
         for unit in range(2, UNITS):
             load_ev(unit, 1)
 
@@ -272,6 +273,7 @@ def tile_generator_pa_t_e_kernel(tc, Pb, Ev, W_pie_words, W_pie_scales, feat, ou
             quantised.append(transpose_and_quantise(unit))
         load_w_words(0)
         load_pb(0)
+        load_w_scales(PASSES, C_COUNT * PASSES)
         for c in range(1, C_COUNT):
             load_w_words(c)
             load_pb(c)

@@ -108,7 +108,6 @@ def tile_generator_pa_t_e_kernel(tc, Pb, Ev, W_pie_words, W_pie_scales, feat, ou
 
         load_ev(0, 2)
         load_ev(1, 1)
-        load_w_scales(0, PASSES)
         for unit in range(2, UNITS):
             load_ev(unit, 1)
 
@@ -271,6 +270,7 @@ def tile_generator_pa_t_e_kernel(tc, Pb, Ev, W_pie_words, W_pie_scales, feat, ou
         quantised = []
         for unit in range(UNITS):
             quantised.append(transpose_and_quantise(unit))
+        load_w_scales(0, PASSES)
         load_w_words(0)
         load_pb(0)
         load_w_scales(PASSES, C_COUNT * PASSES)

@@ -24,6 +24,7 @@ PASSES = ROW // K_PASS
 J_UNIT = 512
 HALVES = ROW // J_UNIT
 UNITS = C_COUNT * HALVES
+UNITS_FIRST = 3
 ROWS_PER_PARTITION = J_UNIT // P
 I_TILES = ROW // P
 I_TILES_PER_LOAD = 2
@@ -108,7 +109,7 @@ def tile_generator_pa_t_e_kernel(tc, Pb, Ev, W_pie_words, W_pie_scales, feat, ou
 
         load_ev(0, 2)
         load_ev(1, 1)
-        for unit in range(2, UNITS):
+        for unit in range(2, UNITS_FIRST):
             load_ev(unit, 1)
 
         d_parts = resident.tile([P, C_COUNT * I_TILES, HALVES + 1], F32, name="d_parts")
@@ -268,28 +269,33 @@ def tile_generator_pa_t_e_kernel(tc, Pb, Ev, W_pie_words, W_pie_scales, feat, ou
             nc.sync.dma_start(out=out_rows[c, :, tiles, :], in_=out_sb[c][:, tiles, :])
 
         quantised = []
-        for unit in range(UNITS):
+        for unit in range(UNITS_FIRST):
             quantised.append(transpose_and_quantise(unit))
         load_w_scales(0, PASSES)
         load_w_words(0)
         load_pb(0)
-        load_w_scales(PASSES, C_COUNT * PASSES)
-        for c in range(1, C_COUNT):
-            load_w_words(c)
-            load_pb(c)
-            load_feat(c - 1)
-        load_feat(C_COUNT - 1)
+        for unit in range(UNITS_FIRST, UNITS):
+            load_ev(unit, 1)
 
         out_sb = []
-        for c in range(C_COUNT):
-            out_tile = ev_or_out.tile([P, I_TILES, COL], F32, name="out%d" % c, tag="ev_or_out")
-            out_sb.append(out_tile)
 
         steps = [(c, t) for c in range(C_COUNT) for t in range(0, I_TILES, I_TILES_PER_LOAD)]
         started = []
         spread_sb = {}
         for step, (c, first_tile) in enumerate(steps):
             step_in_c = first_tile // I_TILES_PER_LOAD
+            if step_in_c == 0:
+                if c == 1:
+                    for unit in range(UNITS_FIRST, UNITS):
+                        quantised.append(transpose_and_quantise(unit))
+                    load_w_scales(PASSES, C_COUNT * PASSES)
+                    for later_c in range(1, C_COUNT):
+                        load_w_words(later_c)
+                        load_pb(later_c)
+                        load_feat(later_c - 1)
+                    load_feat(C_COUNT - 1)
+                out_tile = ev_or_out.tile([P, I_TILES, COL], F32, name="out%d" % c, tag="ev_or_out")
+                out_sb.append(out_tile)
             newly_started = []
             for t in range(first_tile, first_tile + I_TILES_PER_LOAD):
                 for h in range(HALVES):

@@ -51,7 +51,7 @@ def tile_generator_pa_t_e_kernel(tc, Pb, Ev, W_pie_words, W_pie_scales, feat, ou
         ev_or_out = ctx.enter_context(tc.tile_pool(name="ev_or_out", bufs=UNITS))
         staging = ctx.enter_context(tc.tile_pool(name="staging", bufs=4))
         products = ctx.enter_context(tc.tile_pool(name="products", bufs=8))
-        elsewhere = ctx.enter_context(tc.tile_pool(name="elsewhere", bufs=2))
+        elsewhere = ctx.enter_context(tc.tile_pool(name="elsewhere", bufs=4))
         psum = ctx.enter_context(tc.psum_pool(name="psum", bufs=8))
         ctx.enter_context(tc.manual_schedule())
 
@@ -191,10 +191,9 @@ def tile_generator_pa_t_e_kernel(tc, Pb, Ev, W_pie_words, W_pie_scales, feat, ou
             )
 
         def start_reduce_elsewhere(c, t, h, t_transposed):
-            t_copy = elsewhere.tile([P, J_UNIT], F32, name="t_copy")
-            nc.scalar.copy(out=t_copy[:], in_=t_transposed[:])
             t_product = elsewhere.tile([P, J_UNIT], F32, name="t_product")
-            nc.gpsimd.tensor_tensor(out=t_product[:], in0=t_copy[:], in1=pb_half(c, t, h), op=MULT)
+            nc.scalar.copy(out=t_product[:], in_=t_transposed[:])
+            nc.gpsimd.tensor_tensor(out=t_product[:], in0=t_product[:], in1=pb_half(c, t, h), op=MULT)
             return t_product
 
         def finish_reduce_elsewhere(c, t, h, t_product):
@@ -300,8 +299,9 @@ def tile_generator_pa_t_e_kernel(tc, Pb, Ev, W_pie_words, W_pie_scales, feat, ou
             for t in range(first_tile, first_tile + I_TILES_PER_LOAD):
                 for h in range(HALVES):
                     t_transposed = multiply(c, t, h, quantised[c * HALVES + h])
-                    last_bank = t == first_tile + I_TILES_PER_LOAD - 1 and h == HALVES - 1
-                    if last_bank and step_in_c < 3 and step < len(steps) - 2:
+                    last_bank = t == first_tile + I_TILES_PER_LOAD - 1 and h == HALVES - 1 and step_in_c < 3
+                    second_bank = t == first_tile and h == HALVES - 1 and step_in_c == 0 and c < C_COUNT - 1
+                    if (last_bank or second_bank) and step < len(steps) - 2:
                         newly_started.append((c, t, h, start_reduce_elsewhere(c, t, h, t_transposed)))
                     else:
                         reduce_on_vector(c, t, h, t_transposed)
@@ -317,12 +317,14 @@ def tile_generator_pa_t_e_kernel(tc, Pb, Ev, W_pie_words, W_pie_scales, feat, ou
             for args in started:
                 finish_reduce_elsewhere(*args)
             started = newly_started
-            if c >= 1 and step_in_c == 1:
-                scale_runs(c - 1, 0, 4)
-                store_runs(c - 1, 0, 4)
-            if c >= 1 and step_in_c == 2:
-                scale_runs(c - 1, 4, 8)
-                store_runs(c - 1, 4, 8)
+            if c >= 1:
+                shares = ((0, 0), (0, 4), (4, 8), (8, 8)) if c == C_COUNT - 1 else ((0, 0), (0, 1), (1, 4), (4, 8))
+                first, last = shares[step_in_c]
+                scale_runs(c - 1, first, last)
+                if first < 4 <= last:
+                    store_runs(c - 1, 0, 4)
+                if first < 8 <= last:
+                    store_runs(c - 1, 4, 8)
             if c == C_COUNT - 1 and step_in_c == 2:
                 scale_tile(c, 0)
                 scale_tile(c, 1)

@@ -287,10 +287,12 @@ def tile_generator_pa_t_e_kernel(tc, Pb, Ev, W_pie_words, W_pie_scales, feat, ou
                 if c == 1:
                     for unit in range(UNITS_FIRST, UNITS):
                         quantised.append(transpose_and_quantise(unit))
-                    load_w_scales(PASSES, C_COUNT * PASSES)
+                    load_w_scales(PASSES, 2 * PASSES)
                     for later_c in range(1, C_COUNT):
                         load_w_words(later_c)
                         load_pb(later_c)
+                        if later_c == 1:
+                            load_w_scales(2 * PASSES, C_COUNT * PASSES)
                         load_feat(later_c - 1)
                     load_feat(C_COUNT - 1)
                 out_tile = ev_or_out.tile([P, I_TILES, COL], F32, name="out%d" % c, tag="ev_or_out")

@@ -24,7 +24,10 @@ PASSES = ROW // K_PASS
 J_UNIT = 512
 HALVES = ROW // J_UNIT
 UNITS = C_COUNT * HALVES
-UNITS_FIRST = 3
+UNITS_FIRST = 2
+BANKS_PER_STEP = 4
+STEP_OF_UNIT = {2: 2, 3: 3, 4: 5, 5: 7, 6: 9, 7: 11}
+SORT_AHEAD = 4
 ROWS_PER_PARTITION = J_UNIT // P
 I_TILES = ROW // P
 I_TILES_PER_LOAD = 2
@@ -49,6 +52,9 @@ def tile_generator_pa_t_e_kernel(tc, Pb, Ev, W_pie_words, W_pie_scales, feat, ou
     with ExitStack() as ctx:
         resident = ctx.enter_context(tc.tile_pool(name="resident", bufs=1))
         ev_or_out = ctx.enter_context(tc.tile_pool(name="ev_or_out", bufs=UNITS))
+        pb_ring = ctx.enter_context(tc.tile_pool(name="pb_ring", bufs=13))
+        quantised_ring = ctx.enter_context(tc.tile_pool(name="quantised_ring", bufs=4))
+        sorted_ring = ctx.enter_context(tc.tile_pool(name="sorted_ring", bufs=4))
         staging = ctx.enter_context(tc.tile_pool(name="staging", bufs=4))
         products = ctx.enter_context(tc.tile_pool(name="products", bufs=8))
         elsewhere = ctx.enter_context(tc.tile_pool(name="elsewhere", bufs=4))
@@ -86,9 +92,9 @@ def tile_generator_pa_t_e_kernel(tc, Pb, Ev, W_pie_words, W_pie_scales, feat, ou
                 nc.sync.dma_start(out=flat[:, columns], in_=ev_rows[c, h][:, columns])
             ev_sb.append(ev_tile)
 
-        def load_pb(c):
-            for t in range(0, I_TILES, I_TILES_PER_LOAD):
-                pb_tile = resident.tile([P, I_TILES_PER_LOAD, ROW], BF16, name="pb%d_%d" % (c, t))
+        def load_pb(c, first_tile, last_tile):
+            for t in range(first_tile, last_tile, I_TILES_PER_LOAD):
+                pb_tile = pb_ring.tile([P, I_TILES_PER_LOAD, ROW], BF16, name="pb")
                 nc.sync.dma_start(out=pb_tile[:], in_=pb_rows[c, :, t : t + I_TILES_PER_LOAD, :])
                 pb_sb.append(pb_tile)
 
@@ -107,54 +113,82 @@ def tile_generator_pa_t_e_kernel(tc, Pb, Ev, W_pie_words, W_pie_scales, feat, ou
             nc.sync.dma_start(out=feat_tile[:], in_=feat_runs[c] if c < MOVED else feat_rows[c])
             feat_sb.append(feat_tile)
 
-        load_ev(0, 2)
-        load_ev(1, 1)
-        for unit in range(2, UNITS_FIRST):
-            load_ev(unit, 1)
+        load_ev(0, 4)
+        load_ev(1, 2)
+        load_w_scales(0, PASSES)
+        load_w_words(0)
+        load_pb(0, 0, 2)
+        load_ev(2, 2)
+        load_pb(0, 2, 4)
+        load_ev(3, 2)
+        load_pb(0, 4, 8)
+        for c in range(1, C_COUNT):
+            if c == 1:
+                load_w_scales(PASSES, 2 * PASSES)
+            if c == 2:
+                load_w_scales(2 * PASSES, C_COUNT * PASSES)
+            load_w_words(c)
+            if c < C_COUNT - 1:
+                load_pb(c, 0, 2)
+                load_ev(HALVES * (c + 1), 1)
+                load_pb(c, 2, 4)
+                load_ev(HALVES * (c + 1) + 1, 1)
+                load_pb(c, 4, 6)
+                load_feat(c - 1)
+                load_pb(c, 6, 8)
+            else:
+                load_pb(c, 0, 8)
+        load_feat(C_COUNT - 2)
+        load_feat(C_COUNT - 1)
 
         d_parts = resident.tile([P, C_COUNT * I_TILES, HALVES + 1], F32, name="d_parts")
         nc.vector.memset(d_parts[:], 1.0)
         factor = resident.tile([P, C_COUNT * I_TILES], F32, name="factor")
 
-        def transpose_and_quantise(unit):
+        quantised = {}
+        grouped_sb = {}
+        sorted_sb = {}
+
+        def sort_words(unit, g):
             ev_words = ev_sb[unit][:].bitcast(F32)
-            grouped = []
-            grouped_words = []
-            for g in range(PASSES):
-                grouped_g = staging.tile([P, 4 * J_UNIT], BF16, name="grouped", align_bytes=64)
-                grouped.append(grouped_g)
-                grouped_words.append(
-                    grouped_g[:].bitcast(F32).rearrange("p (r a_pair x) -> p r a_pair x", a_pair=2, x=4)
-                )
-            codes = resident.tile([P, PASSES, J_UNIT], U32, name="codes%d" % unit, align_bytes=64)
-            planes = resident.tile([P, PASSES, J_UNIT], U8, name="planes%d" % unit, align_bytes=64)
+            sorted_words = sorted_ring.tile([P, 2, ROWS_PER_PARTITION, P], F32, name="sorted_words")
+            nc.scalar.copy(
+                out=sorted_words[:],
+                in_=ev_words[:, :, 2 * P * g : 2 * P * (g + 1)].rearrange("r a (w s) -> r s a w", s=2),
+            )
+            sorted_sb[unit, g] = sorted_words
+
+        def transpose_pass(unit, g):
+            ev_words = ev_sb[unit][:].bitcast(F32)
+            grouped = staging.tile([P, 4 * J_UNIT], BF16, name="grouped", align_bytes=64)
+            grouped_words = grouped[:].bitcast(F32).rearrange("p (r a_pair x) -> p r a_pair x", a_pair=2, x=4)
             for a_pair in range(2):
-                for g in range(PASSES):
-                    transposed = psum.tile([P, 4, P], F32, name="transposed", tag="bank")
-                    for a_low in range(2):
-                        for s in range(2):
-                            nc.tensor.transpose(
-                                transposed[:, 2 * a_low + s, :],
-                                ev_words[:, 2 * a_pair + a_low, 256 * g + s : 256 * (g + 1) : 2],
-                                identity[:],
-                            )
-                    if a_pair == 1 and g == PASSES - 1:
-                        nc.vector.tensor_copy(
-                            out=grouped_words[g][:, :, a_pair, :],
-                            in_=transposed[:].rearrange("p x r -> p r x"),
-                        )
-                    else:
-                        nc.scalar.copy(
-                            out=grouped_words[g][:, :, a_pair, :],
-                            in_=transposed[:].rearrange("p x r -> p r x"),
-                        )
-            for g in range(PASSES):
-                nc.vector.quantize_mx(
-                    out=codes[:, g, :].bitcast(FP8X4),
-                    scales=planes[:, g, :],
-                    in_=grouped[g][:],
+                transposed = psum.tile([P, 4, P], F32, name="transposed", tag="bank")
+                for a_low in range(2):
+                    a = 2 * a_pair + a_low
+                    for s in range(2):
+                        if unit < UNITS_FIRST:
+                            words = ev_words[:, a, 2 * P * g + s : 2 * P * (g + 1) : 2]
+                        else:
+                            words = sorted_sb[unit, g][:, s, a, :]
+                        nc.tensor.transpose(transposed[:, 2 * a_low + s, :], words, identity[:])
+                nc.scalar.copy(
+                    out=grouped_words[:, :, a_pair, :],
+                    in_=transposed[:].rearrange("p x r -> p r x"),
                 )
-            return codes, planes
+            grouped_sb[unit, g] = grouped
+
+        def quantise_pass(unit, g):
+            if g == 0:
+                codes = quantised_ring.tile([P, PASSES, J_UNIT], U32, name="codes", align_bytes=64)
+                planes = quantised_ring.tile([P, PASSES, J_UNIT], U8, name="planes", align_bytes=64)
+                quantised[unit] = codes, planes
+            codes, planes = quantised[unit]
+            nc.vector.quantize_mx(
+                out=codes[:, g, :].bitcast(FP8X4),
+                scales=planes[:, g, :],
+                in_=grouped_sb[unit, g][:],
+            )
 
         def multiply(c, t, h, quantised_ev):
             codes, planes = quantised_ev
@@ -267,58 +301,60 @@ def tile_generator_pa_t_e_kernel(tc, Pb, Ev, W_pie_words, W_pie_scales, feat, ou
             tiles = slice(first_tile, first_tile + I_TILES_PER_LOAD)
             nc.sync.dma_start(out=out_rows[c, :, tiles, :], in_=out_sb[c][:, tiles, :])
 
-        quantised = []
         for unit in range(UNITS_FIRST):
-            quantised.append(transpose_and_quantise(unit))
-        load_w_scales(0, PASSES)
-        load_w_words(0)
-        load_pb(0)
+            for g in range(PASSES):
+                transpose_pass(unit, g)
+            for g in range(PASSES):
+                quantise_pass(unit, g)
+
+        sorts_before = {}
+        transposes_before = {}
+        quantises_before = {}
         for unit in range(UNITS_FIRST, UNITS):
-            load_ev(unit, 1)
+            bank = BANKS_PER_STEP * STEP_OF_UNIT[unit]
+            transposes_before[bank] = unit
+            for g in range(PASSES):
+                sorts_before[bank - SORT_AHEAD + 2 * g] = (unit, g)
+                quantises_before[bank + 1 + g] = (unit, g)
 
         out_sb = []
-
         steps = [(c, t) for c in range(C_COUNT) for t in range(0, I_TILES, I_TILES_PER_LOAD)]
         started = []
         spread_sb = {}
+        bank = 0
         for step, (c, first_tile) in enumerate(steps):
             step_in_c = first_tile // I_TILES_PER_LOAD
             if step_in_c == 0:
-                if c == 1:
-                    for unit in range(UNITS_FIRST, UNITS):
-                        quantised.append(transpose_and_quantise(unit))
-                    load_w_scales(PASSES, 2 * PASSES)
-                    for later_c in range(1, C_COUNT):
-                        load_w_words(later_c)
-                        load_pb(later_c)
-                        if later_c == 1:
-                            load_w_scales(2 * PASSES, C_COUNT * PASSES)
-                        load_feat(later_c - 1)
-                    load_feat(C_COUNT - 1)
                 out_tile = ev_or_out.tile([P, I_TILES, COL], F32, name="out%d" % c, tag="ev_or_out")
                 out_sb.append(out_tile)
-            newly_started = []
             for t in range(first_tile, first_tile + I_TILES_PER_LOAD):
                 for h in range(HALVES):
+                    if bank in sorts_before:
+                        sort_words(*sorts_before[bank])
+                    if bank in quantises_before:
+                        quantise_pass(*quantises_before[bank])
+                    if bank in transposes_before:
+                        for g in range(PASSES):
+                            transpose_pass(transposes_before[bank], g)
                     t_transposed = multiply(c, t, h, quantised[c * HALVES + h])
-                    last_bank = t == first_tile + I_TILES_PER_LOAD - 1 and h == HALVES - 1 and step_in_c < 3
-                    second_bank = t == first_tile and h == HALVES - 1 and step_in_c == 0 and c < C_COUNT - 1
-                    if (last_bank or second_bank) and step < len(steps) - 2:
-                        newly_started.append((c, t, h, start_reduce_elsewhere(c, t, h, t_transposed)))
+                    if bank in (51, 55, 57):
+                        started.append((bank, (c, t, h, start_reduce_elsewhere(c, t, h, t_transposed))))
                     else:
                         reduce_on_vector(c, t, h, t_transposed)
-                if t == first_tile:
-                    if c >= 1 and step_in_c == 0:
-                        spread_sb[c - 1] = spread_factors(c - 1)
-                    if c >= 1 and step_in_c == 1:
-                        move_factors(c - 1, spread_sb[c - 1])
-                    if c == C_COUNT - 1 and step_in_c == 2:
-                        make_factors(c, 0, 2)
-                    if c == C_COUNT - 1 and step_in_c == 3:
-                        make_factors(c, 2, 5)
-            for args in started:
-                finish_reduce_elsewhere(*args)
-            started = newly_started
+                    while started and started[0][0] <= bank - 4:
+                        finish_reduce_elsewhere(*started[0][1])
+                        started = started[1:]
+                    if t == first_tile + 1 and h == HALVES - 1 and c >= 1:
+                        if step_in_c == 0:
+                            spread_sb[c - 1] = spread_factors(c - 1)
+                        if step_in_c == 1:
+                            move_factors(c - 1, spread_sb[c - 1])
+                    if t == first_tile and h == HALVES - 1 and c == C_COUNT - 1:
+                        if step_in_c == 2:
+                            make_factors(c, 0, 2)
+                        if step_in_c == 3:
+                            make_factors(c, 2, 5)
+                    bank += 1
             if c >= 1:
                 shares = ((0, 0), (0, 4), (4, 8), (8, 8)) if c == C_COUNT - 1 else ((0, 0), (0, 1), (1, 4), (4, 8))
                 first, last = shares[step_in_c]

@@ -25,8 +25,9 @@ J_UNIT = 512
 HALVES = ROW // J_UNIT
 UNITS = C_COUNT * HALVES
 UNITS_FIRST = 2
-BANKS_PER_STEP = 4
-STEP_OF_UNIT = {2: 2, 3: 3, 4: 5, 5: 7, 6: 9, 7: 11}
+BANKS_PER_C = 16
+TRANSPOSE_AT = (3, 8)
+FIRST_DELAY = 3
 SORT_AHEAD = 4
 ROWS_PER_PARTITION = J_UNIT // P
 I_TILES = ROW // P
@@ -118,27 +119,26 @@ def tile_generator_pa_t_e_kernel(tc, Pb, Ev, W_pie_words, W_pie_scales, feat, ou
         load_w_scales(0, PASSES)
         load_w_words(0)
         load_pb(0, 0, 2)
-        load_ev(2, 2)
+        load_ev(2, 1)
         load_pb(0, 2, 4)
-        load_ev(3, 2)
-        load_pb(0, 4, 8)
+        load_ev(3, 1)
+        load_pb(0, 4, 6)
+        load_w_scales(PASSES, 2 * PASSES)
+        load_pb(0, 6, 8)
         for c in range(1, C_COUNT):
-            if c == 1:
-                load_w_scales(PASSES, 2 * PASSES)
-            if c == 2:
-                load_w_scales(2 * PASSES, C_COUNT * PASSES)
             load_w_words(c)
             if c < C_COUNT - 1:
-                load_pb(c, 0, 2)
                 load_ev(HALVES * (c + 1), 1)
-                load_pb(c, 2, 4)
+                load_pb(c, 0, 4)
                 load_ev(HALVES * (c + 1) + 1, 1)
-                load_pb(c, 4, 6)
                 load_feat(c - 1)
-                load_pb(c, 6, 8)
             else:
-                load_pb(c, 0, 8)
-        load_feat(C_COUNT - 2)
+                load_pb(c, 0, 4)
+                load_feat(c - 1)
+            load_pb(c, 4, 6)
+            if c == 1:
+                load_w_scales(2 * PASSES, C_COUNT * PASSES)
+            load_pb(c, 6, 8)
         load_feat(C_COUNT - 1)
 
         d_parts = resident.tile([P, C_COUNT * I_TILES, HALVES + 1], F32, name="d_parts")
@@ -311,7 +311,8 @@ def tile_generator_pa_t_e_kernel(tc, Pb, Ev, W_pie_words, W_pie_scales, feat, ou
         transposes_before = {}
         quantises_before = {}
         for unit in range(UNITS_FIRST, UNITS):
-            bank = BANKS_PER_STEP * STEP_OF_UNIT[unit]
+            c, h = divmod(unit, HALVES)
+            bank = BANKS_PER_C * (c - 1) + TRANSPOSE_AT[h] + (FIRST_DELAY if c == 1 else 0)
             transposes_before[bank] = unit
             for g in range(PASSES):
                 sorts_before[bank - SORT_AHEAD + 2 * g] = (unit, g)
@@ -337,11 +338,11 @@ def tile_generator_pa_t_e_kernel(tc, Pb, Ev, W_pie_words, W_pie_scales, feat, ou
                         for g in range(PASSES):
                             transpose_pass(transposes_before[bank], g)
                     t_transposed = multiply(c, t, h, quantised[c * HALVES + h])
-                    if bank in (51, 55, 57):
+                    if bank in (49, 51, 54, 57):
                         started.append((bank, (c, t, h, start_reduce_elsewhere(c, t, h, t_transposed))))
                     else:
                         reduce_on_vector(c, t, h, t_transposed)
-                    while started and started[0][0] <= bank - 4:
+                    while started and started[0][0] <= bank - 3:
                         finish_reduce_elsewhere(*started[0][1])
                         started = started[1:]
                     if t == first_tile + 1 and h == HALVES - 1 and c >= 1:

@@ -26,9 +26,12 @@ HALVES = ROW // J_UNIT
 UNITS = C_COUNT * HALVES
 UNITS_FIRST = 2
 BANKS_PER_C = 16
-TRANSPOSE_AT = (3, 8)
-FIRST_DELAY = 3
-SORT_AHEAD = 4
+TRANSPOSE_AT = (3, 10)
+TRANSPOSE_AT_FIRST = (5, 12)
+SORT_AHEAD = 6
+FINISH_AFTER = 5
+ELSEWHERE = (6,)
+ELSEWHERE_LAST = (0, 4, 8)
 ROWS_PER_PARTITION = J_UNIT // P
 I_TILES = ROW // P
 I_TILES_PER_LOAD = 2
@@ -118,23 +121,20 @@ def tile_generator_pa_t_e_kernel(tc, Pb, Ev, W_pie_words, W_pie_scales, feat, ou
         load_ev(1, 2)
         load_w_scales(0, PASSES)
         load_w_words(0)
-        load_pb(0, 0, 2)
         load_ev(2, 1)
-        load_pb(0, 2, 4)
+        load_pb(0, 0, 4)
         load_ev(3, 1)
         load_pb(0, 4, 6)
         load_w_scales(PASSES, 2 * PASSES)
         load_pb(0, 6, 8)
         for c in range(1, C_COUNT):
-            load_w_words(c)
             if c < C_COUNT - 1:
                 load_ev(HALVES * (c + 1), 1)
-                load_pb(c, 0, 4)
+            load_w_words(c)
+            load_pb(c, 0, 4)
+            if c < C_COUNT - 1:
                 load_ev(HALVES * (c + 1) + 1, 1)
-                load_feat(c - 1)
-            else:
-                load_pb(c, 0, 4)
-                load_feat(c - 1)
+            load_feat(c - 1)
             load_pb(c, 4, 6)
             if c == 1:
                 load_w_scales(2 * PASSES, C_COUNT * PASSES)
@@ -172,10 +172,8 @@ def tile_generator_pa_t_e_kernel(tc, Pb, Ev, W_pie_words, W_pie_scales, feat, ou
                         else:
                             words = sorted_sb[unit, g][:, s, a, :]
                         nc.tensor.transpose(transposed[:, 2 * a_low + s, :], words, identity[:])
-                nc.scalar.copy(
-                    out=grouped_words[:, :, a_pair, :],
-                    in_=transposed[:].rearrange("p x r -> p r x"),
-                )
+                copy = nc.vector.tensor_copy if unit < UNITS_FIRST and a_pair == 1 else nc.scalar.copy
+                copy(out=grouped_words[:, :, a_pair, :], in_=transposed[:].rearrange("p x r -> p r x"))
             grouped_sb[unit, g] = grouped
 
         def quantise_pass(unit, g):
@@ -312,10 +310,10 @@ def tile_generator_pa_t_e_kernel(tc, Pb, Ev, W_pie_words, W_pie_scales, feat, ou
         quantises_before = {}
         for unit in range(UNITS_FIRST, UNITS):
             c, h = divmod(unit, HALVES)
-            bank = BANKS_PER_C * (c - 1) + TRANSPOSE_AT[h] + (FIRST_DELAY if c == 1 else 0)
+            bank = BANKS_PER_C * (c - 1) + (TRANSPOSE_AT_FIRST if c == 1 else TRANSPOSE_AT)[h]
             transposes_before[bank] = unit
             for g in range(PASSES):
-                sorts_before[bank - SORT_AHEAD + 2 * g] = (unit, g)
+                sorts_before[max(0, bank - SORT_AHEAD + 2 * g)] = (unit, g)
                 quantises_before[bank + 1 + g] = (unit, g)
 
         out_sb = []
@@ -328,8 +326,11 @@ def tile_generator_pa_t_e_kernel(tc, Pb, Ev, W_pie_words, W_pie_scales, feat, ou
             if step_in_c == 0:
                 out_tile = ev_or_out.tile([P, I_TILES, COL], F32, name="out%d" % c, tag="ev_or_out")
                 out_sb.append(out_tile)
-            for t in range(first_tile, first_tile + I_TILES_PER_LOAD):
-                for h in range(HALVES):
+            pair = [(first_tile + t, h) for t in range(I_TILES_PER_LOAD) for h in range(HALVES)]
+            if c < C_COUNT - 1:
+                pair = [(first_tile + t, h) for h in range(HALVES) for t in range(I_TILES_PER_LOAD)]
+            for t, h in pair:
+                if True:
                     if bank in sorts_before:
                         sort_words(*sorts_before[bank])
                     if bank in quantises_before:
@@ -338,23 +339,21 @@ def tile_generator_pa_t_e_kernel(tc, Pb, Ev, W_pie_words, W_pie_scales, feat, ou
                         for g in range(PASSES):
                             transpose_pass(transposes_before[bank], g)
                     t_transposed = multiply(c, t, h, quantised[c * HALVES + h])
-                    if bank in (49, 51, 54, 57):
+                    if bank % BANKS_PER_C in (ELSEWHERE_LAST if c == C_COUNT - 1 else ELSEWHERE):
                         started.append((bank, (c, t, h, start_reduce_elsewhere(c, t, h, t_transposed))))
                     else:
                         reduce_on_vector(c, t, h, t_transposed)
-                    while started and started[0][0] <= bank - 3:
+                    while started and started[0][0] <= bank - FINISH_AFTER:
                         finish_reduce_elsewhere(*started[0][1])
                         started = started[1:]
-                    if t == first_tile + 1 and h == HALVES - 1 and c >= 1:
-                        if step_in_c == 0:
-                            spread_sb[c - 1] = spread_factors(c - 1)
-                        if step_in_c == 1:
-                            move_factors(c - 1, spread_sb[c - 1])
-                    if t == first_tile and h == HALVES - 1 and c == C_COUNT - 1:
-                        if step_in_c == 2:
-                            make_factors(c, 0, 2)
-                        if step_in_c == 3:
-                            make_factors(c, 2, 5)
+                    if c >= 1 and bank % BANKS_PER_C == 1:
+                        spread_sb[c - 1] = spread_factors(c - 1)
+                    if c >= 1 and bank % BANKS_PER_C == 5:
+                        move_factors(c - 1, spread_sb[c - 1])
+                    if bank == 57:
+                        make_factors(c, 0, 2)
+                    if bank == 61:
+                        make_factors(c, 2, 5)
                     bank += 1
             if c >= 1:
                 shares = ((0, 0), (0, 4), (4, 8), (8, 8)) if c == C_COUNT - 1 else ((0, 0), (0, 1), (1, 4), (4, 8))

from contextlib import ExitStack

import concourse.mybir as mybir
from concourse.masks import make_identity

F32 = mybir.dt.float32
BF16 = mybir.dt.bfloat16
U8 = mybir.dt.uint8
U32 = mybir.dt.uint32
I32 = mybir.dt.int32
FP8X4 = mybir.dt.float8_e4m3fn_x4
FP4X4 = mybir.dt.float4_e2m1fn_x4
MULT = mybir.AluOpType.mult
ADD = mybir.AluOpType.add
COPY = mybir.ActivationFunctionType.Copy
AXIS_X = mybir.AxisListType.X

P = 128
C_COUNT = 4
ROW = 1024
COL = 256
K_PASS = 4 * P
PASSES = ROW // K_PASS
J_UNIT = 512
HALVES = ROW // J_UNIT
UNITS = C_COUNT * HALVES
UNITS_FIRST = 2
BANKS_PER_C = 16
TRANSPOSE_AT = (3, 10)
TRANSPOSE_AT_FIRST = (5, 12)
SORT_AHEAD = 6
FINISH_AFTER = 5
ELSEWHERE = (6,)
ELSEWHERE_LAST = (0, 4, 8)
ROWS_PER_PARTITION = J_UNIT // P
I_TILES = ROW // P
I_TILES_PER_LOAD = 2
RESIDUAL_SCALE = 0.3
MOVED = C_COUNT - 1

FLOPS = 2 * C_COUNT * ROW * ROW * ROW


def tile_generator_pa_t_e_kernel(tc, Pb, Ev, W_pie_words, W_pie_scales, feat, out):
    nc = tc.nc

    ev_rows = Ev.rearrange("c (h r a) k -> c h r (a k)", h=HALVES, a=ROWS_PER_PARTITION)
    pb_rows = Pb.rearrange("c (t p) j -> c p t j", p=P)
    feat_rows = feat.rearrange("c (t p) f -> c p t f", p=P)
    out_rows = out.rearrange("c (t p) f -> c p t f", p=P)
    feat_runs = feat.rearrange("c (p a) f -> c p a f", a=I_TILES)
    out_runs = out.rearrange("c (p a) f -> c p a f", a=I_TILES)
    w_word_rows = W_pie_words.bitcast(I32).rearrange("g p w -> p g w")
    w_scale_rows = W_pie_scales.bitcast(I32).rearrange("g q n -> q g n")

    with ExitStack() as ctx:
        resident = ctx.enter_context(tc.tile_pool(name="resident", bufs=1))
        ev_or_out = ctx.enter_context(tc.tile_pool(name="ev_or_out", bufs=UNITS))
        pb_ring = ctx.enter_context(tc.tile_pool(name="pb_ring", bufs=13))
        quantised_ring = ctx.enter_context(tc.tile_pool(name="quantised_ring", bufs=4))
        sorted_ring = ctx.enter_context(tc.tile_pool(name="sorted_ring", bufs=4))
        staging = ctx.enter_context(tc.tile_pool(name="staging", bufs=4))
        products = ctx.enter_context(tc.tile_pool(name="products", bufs=8))
        elsewhere = ctx.enter_context(tc.tile_pool(name="elsewhere", bufs=4))
        psum = ctx.enter_context(tc.psum_pool(name="psum", bufs=8))
        ctx.enter_context(tc.manual_schedule())

        identity = resident.tile([P, P], F32, name="identity")
        make_identity(nc, identity[:])

        group_of = resident.tile([P, P // I_TILES], F32, name="group_of")
        nc.vector.tensor_reduce(
            out=group_of[:], in_=identity[:].rearrange("p (q a) -> p q a", a=I_TILES), axis=AXIS_X, op=ADD
        )
        place_in_group = resident.tile([P, I_TILES], F32, name="place_in_group")
        nc.vector.tensor_reduce(
            out=place_in_group[:], in_=identity[:].rearrange("p (q a) -> p a q", a=I_TILES), axis=AXIS_X, op=ADD
        )

        w_planes = resident.tile([P, C_COUNT * PASSES, ROW], U8, name="w_planes", align_bytes=64)
        w_planes_i32 = w_planes[:].bitcast(I32)
        nc.vector.memset(w_planes_i32, 0)

        ev_sb = []
        pb_sb = []
        w_sb = []
        feat_sb = []

        def load_ev(unit, pieces):
            c, h = divmod(unit, HALVES)
            ev_tile = ev_or_out.tile([P, ROWS_PER_PARTITION, ROW], BF16, name="ev%d" % unit, tag="ev_or_out")
            flat = ev_tile[:].rearrange("p a k -> p (a k)")
            width = ROWS_PER_PARTITION * ROW // pieces
            for piece in range(pieces):
                columns = slice(piece * width, (piece + 1) * width)
                nc.sync.dma_start(out=flat[:, columns], in_=ev_rows[c, h][:, columns])
            ev_sb.append(ev_tile)

        def load_pb(c, first_tile, last_tile):
            for t in range(first_tile, last_tile, I_TILES_PER_LOAD):
                pb_tile = pb_ring.tile([P, I_TILES_PER_LOAD, ROW], BF16, name="pb")
                nc.sync.dma_start(out=pb_tile[:], in_=pb_rows[c, :, t : t + I_TILES_PER_LOAD, :])
                pb_sb.append(pb_tile)

        def load_w_scales(first_pass, last_pass):
            some_passes = slice(first_pass, last_pass)
            for r in range(4):
                nc.sync.dma_start(out=w_planes_i32[r:P:32, some_passes, :], in_=w_scale_rows[r:16:4, some_passes, :])

        def load_w_words(c):
            w_tile = resident.tile([P, PASSES, 2 * ROW], U8, name="w%d" % c, align_bytes=64)
            nc.sync.dma_start(out=w_tile[:].bitcast(I32), in_=w_word_rows[:, PASSES * c : PASSES * (c + 1), :])
            w_sb.append(w_tile)

        def load_feat(c):
            feat_tile = ev_or_out.tile([P, I_TILES, COL], BF16, name="feat%d" % c, tag="ev_or_out")
            nc.sync.dma_start(out=feat_tile[:], in_=feat_runs[c] if c < MOVED else feat_rows[c])
            feat_sb.append(feat_tile)

        load_ev(0, 4)
        load_ev(1, 2)
        load_w_scales(0, PASSES)
        load_w_words(0)
        load_ev(2, 1)
        load_pb(0, 0, 4)
        load_ev(3, 1)
        load_pb(0, 4, 6)
        load_w_scales(PASSES, 2 * PASSES)
        load_pb(0, 6, 8)
        for c in range(1, C_COUNT):
            if c < C_COUNT - 1:
                load_ev(HALVES * (c + 1), 1)
            load_w_words(c)
            load_pb(c, 0, 4)
            if c < C_COUNT - 1:
                load_ev(HALVES * (c + 1) + 1, 1)
            load_feat(c - 1)
            load_pb(c, 4, 6)
            if c == 1:
                load_w_scales(2 * PASSES, C_COUNT * PASSES)
            load_pb(c, 6, 8)
        load_feat(C_COUNT - 1)

        d_parts = resident.tile([P, C_COUNT * I_TILES, HALVES + 1], F32, name="d_parts")
        nc.vector.memset(d_parts[:], 1.0)
        factor = resident.tile([P, C_COUNT * I_TILES], F32, name="factor")

        quantised = {}
        grouped_sb = {}
        sorted_sb = {}

        def sort_words(unit, g):
            ev_words = ev_sb[unit][:].bitcast(F32)
            sorted_words = sorted_ring.tile([P, 2, ROWS_PER_PARTITION, P], F32, name="sorted_words")
            nc.scalar.copy(
                out=sorted_words[:],
                in_=ev_words[:, :, 2 * P * g : 2 * P * (g + 1)].rearrange("r a (w s) -> r s a w", s=2),
            )
            sorted_sb[unit, g] = sorted_words

        def transpose_pass(unit, g):
            ev_words = ev_sb[unit][:].bitcast(F32)
            grouped = staging.tile([P, 4 * J_UNIT], BF16, name="grouped", align_bytes=64)
            grouped_words = grouped[:].bitcast(F32).rearrange("p (r a_pair x) -> p r a_pair x", a_pair=2, x=4)
            for a_pair in range(2):
                transposed = psum.tile([P, 4, P], F32, name="transposed", tag="bank")
                for a_low in range(2):
                    a = 2 * a_pair + a_low
                    for s in range(2):
                        if unit < UNITS_FIRST:
                            words = ev_words[:, a, 2 * P * g + s : 2 * P * (g + 1) : 2]
                        else:
                            words = sorted_sb[unit, g][:, s, a, :]
                        nc.tensor.transpose(transposed[:, 2 * a_low + s, :], words, identity[:])
                copy = nc.vector.tensor_copy if unit < UNITS_FIRST and a_pair == 1 else nc.scalar.copy
                copy(out=grouped_words[:, :, a_pair, :], in_=transposed[:].rearrange("p x r -> p r x"))
            grouped_sb[unit, g] = grouped

        def quantise_pass(unit, g):
            if g == 0:
                codes = quantised_ring.tile([P, PASSES, J_UNIT], U32, name="codes", align_bytes=64)
                planes = quantised_ring.tile([P, PASSES, J_UNIT], U8, name="planes", align_bytes=64)
                quantised[unit] = codes, planes
            codes, planes = quantised[unit]
            nc.vector.quantize_mx(
                out=codes[:, g, :].bitcast(FP8X4),
                scales=planes[:, g, :],
                in_=grouped_sb[unit, g][:],
            )

        def multiply(c, t, h, quantised_ev):
            codes, planes = quantised_ev
            t_transposed = psum.tile([P, J_UNIT], F32, name="t_transposed", tag="bank")
            for g in range(PASSES):
                nc.tensor.matmul_mx(
                    out=t_transposed[:],
                    lhsT=w_sb[c][:, g, 2 * P * t : 2 * P * (t + 1)].bitcast(FP4X4),
                    lhsT_scale=w_planes[:, PASSES * c + g, P * t : P * (t + 1)],
                    rhs=codes[:, g, :].bitcast(FP8X4),
                    rhs_scale=planes[:, g, :],
                    start=(g == 0),
                    stop=(g == PASSES - 1),
                )
            return t_transposed

        def pb_half(c, t, h):
            pb_tile = pb_sb[(c * I_TILES + t) // I_TILES_PER_LOAD]
            return pb_tile[:, t % I_TILES_PER_LOAD, J_UNIT * h : J_UNIT * (h + 1)]

        def d_column(c, t, h):
            return d_parts[:, c * I_TILES + t, h : h + 1]

        def reduce_on_vector(c, t, h, t_transposed):
            product = products.tile([P, J_UNIT], F32, name="product")
            nc.vector.scalar_tensor_tensor(
                out=product[:],
                in0=t_transposed[:],
                scalar=RESIDUAL_SCALE,
                in1=pb_half(c, t, h),
                op0=MULT,
                op1=MULT,
                accum_out=d_column(c, t, h),
            )

        def start_reduce_elsewhere(c, t, h, t_transposed):
            t_product = elsewhere.tile([P, J_UNIT], F32, name="t_product")
            nc.scalar.copy(out=t_product[:], in_=t_transposed[:])
            nc.gpsimd.tensor_tensor(out=t_product[:], in0=t_product[:], in1=pb_half(c, t, h), op=MULT)
            return t_product

        def finish_reduce_elsewhere(c, t, h, t_product):
            nc.scalar.activation(
                out=t_product[:],
                in_=t_product[:],
                func=COPY,
                scale=RESIDUAL_SCALE,
                accum_out=d_column(c, t, h),
            )

        def make_factors(c, first_tile, tiles):
            columns = slice(c * I_TILES + first_tile, c * I_TILES + first_tile + tiles)
            nc.vector.tensor_reduce(out=factor[:, columns], in_=d_parts[:, columns, :], axis=AXIS_X, op=ADD)

        factor_by_run = resident.tile([P, C_COUNT * I_TILES], F32, name="factor_by_run")

        def spread_factors(c):
            make_factors(c, 0, I_TILES)
            spread = resident.tile([P, I_TILES, P // I_TILES], F32, name="spread%d" % c)
            shape = [P, I_TILES, P // I_TILES]
            nc.vector.tensor_tensor(
                out=spread[:],
                in0=factor[:, c * I_TILES : (c + 1) * I_TILES].unsqueeze(2).to_broadcast(shape),
                in1=group_of[:].unsqueeze(1).to_broadcast(shape),
                op=MULT,
            )
            return spread

        def move_factors(c, spread):
            moved = psum.tile([P, I_TILES], F32, name="moved", tag="bank")
            nc.tensor.matmul(
                out=moved[:],
                lhsT=spread[:].rearrange("p t q -> p (t q)"),
                rhs=place_in_group[:],
                start=True,
                stop=True,
            )
            nc.scalar.copy(out=factor_by_run[:, c * I_TILES : (c + 1) * I_TILES], in_=moved[:])

        def scale_runs(c, first, last):
            for a in range(first, last):
                column = c * I_TILES + a
                nc.scalar.activation(
                    out=out_sb[c][:, a, :],
                    in_=feat_sb[c][:, a, :],
                    func=COPY,
                    scale=factor_by_run[:, column : column + 1],
                )

        def store_runs(c, first, last):
            nc.sync.dma_start(out=out_runs[c, :, first:last, :], in_=out_sb[c][:, first:last, :])

        def scale_tile(c, t, on_vector=False):
            column = c * I_TILES + t
            if on_vector:
                nc.vector.tensor_scalar_mul(
                    out=out_sb[c][:, t, :],
                    in0=feat_sb[c][:, t, :],
                    scalar1=factor[:, column : column + 1],
                )
            else:
                nc.scalar.activation(
                    out=out_sb[c][:, t, :],
                    in_=feat_sb[c][:, t, :],
                    func=COPY,
                    scale=factor[:, column : column + 1],
                )

        def store_pair(c, first_tile):
            tiles = slice(first_tile, first_tile + I_TILES_PER_LOAD)
            nc.sync.dma_start(out=out_rows[c, :, tiles, :], in_=out_sb[c][:, tiles, :])

        for unit in range(UNITS_FIRST):
            for g in range(PASSES):
                transpose_pass(unit, g)
            for g in range(PASSES):
                quantise_pass(unit, g)

        sorts_before = {}
        transposes_before = {}
        quantises_before = {}
        for unit in range(UNITS_FIRST, UNITS):
            c, h = divmod(unit, HALVES)
            bank = BANKS_PER_C * (c - 1) + (TRANSPOSE_AT_FIRST if c == 1 else TRANSPOSE_AT)[h]
            transposes_before[bank] = unit
            for g in range(PASSES):
                sorts_before[max(0, bank - SORT_AHEAD + 2 * g)] = (unit, g)
                quantises_before[bank + 1 + g] = (unit, g)

        out_sb = []
        steps = [(c, t) for c in range(C_COUNT) for t in range(0, I_TILES, I_TILES_PER_LOAD)]
        started = []
        spread_sb = {}
        bank = 0
        for step, (c, first_tile) in enumerate(steps):
            step_in_c = first_tile // I_TILES_PER_LOAD
            if step_in_c == 0:
                out_tile = ev_or_out.tile([P, I_TILES, COL], F32, name="out%d" % c, tag="ev_or_out")
                out_sb.append(out_tile)
            pair = [(first_tile + t, h) for t in range(I_TILES_PER_LOAD) for h in range(HALVES)]
            if c < C_COUNT - 1:
                pair = [(first_tile + t, h) for h in range(HALVES) for t in range(I_TILES_PER_LOAD)]
            for t, h in pair:
                if True:
                    if bank in sorts_before:
                        sort_words(*sorts_before[bank])
                    if bank in quantises_before:
                        quantise_pass(*quantises_before[bank])
                    if bank in transposes_before:
                        for g in range(PASSES):
                            transpose_pass(transposes_before[bank], g)
                    t_transposed = multiply(c, t, h, quantised[c * HALVES + h])
                    if bank % BANKS_PER_C in (ELSEWHERE_LAST if c == C_COUNT - 1 else ELSEWHERE):
                        started.append((bank, (c, t, h, start_reduce_elsewhere(c, t, h, t_transposed))))
                    else:
                        reduce_on_vector(c, t, h, t_transposed)
                    while started and started[0][0] <= bank - FINISH_AFTER:
                        finish_reduce_elsewhere(*started[0][1])
                        started = started[1:]
                    if c >= 1 and bank % BANKS_PER_C == 1:
                        spread_sb[c - 1] = spread_factors(c - 1)
                    if c >= 1 and bank % BANKS_PER_C == 5:
                        move_factors(c - 1, spread_sb[c - 1])
                    if bank == 57:
                        make_factors(c, 0, 2)
                    if bank == 61:
                        make_factors(c, 2, 5)
                    bank += 1
            if c >= 1:
                shares = ((0, 0), (0, 4), (4, 8), (8, 8)) if c == C_COUNT - 1 else ((0, 0), (0, 1), (1, 4), (4, 8))
                first, last = shares[step_in_c]
                scale_runs(c - 1, first, last)
                if first < 4 <= last:
                    store_runs(c - 1, 0, 4)
                if first < 8 <= last:
                    store_runs(c - 1, 4, 8)
            if c == C_COUNT - 1 and step_in_c == 2:
                scale_tile(c, 0)
                scale_tile(c, 1)
                store_pair(c, 0)
            if c == C_COUNT - 1 and step_in_c == 3:
                for pair in (2, 4):
                    scale_tile(c, pair)
                    scale_tile(c, pair + 1)
                    store_pair(c, pair)
                scale_tile(c, 6)
        make_factors(C_COUNT - 1, I_TILES - 1, 1)
        scale_tile(C_COUNT - 1, I_TILES - 1, on_vector=True)
        store_pair(C_COUNT - 1, I_TILES - 2)
